import numpy as np
import ml_dtypes


def mxq(x, axis, fmt="e4m3"):
    dtype, down = {"e4m3": (ml_dtypes.float8_e4m3fn, 7), "e5m2": (ml_dtypes.float8_e5m2, 14)}[fmt]
    v = np.moveaxis(np.asarray(x, np.float32).astype(ml_dtypes.bfloat16).astype(np.float64), axis, -1)
    blocks = v.reshape(v.shape[:-1] + (-1, 32))
    amax = np.abs(blocks).max(-1, keepdims=True)
    byte = np.maximum(np.where(amax > 0, np.frexp(amax)[1] - 1 + 127, 0) - down, 1)
    scale = np.exp2(byte - 127.0)
    codes = (blocks / scale).astype(np.float32).astype(dtype).astype(np.float64)
    return np.moveaxis((codes * scale).reshape(v.shape), -1, axis)


WIDE = False


def mx_kscale(k):
    if not WIDE:
        return np.ones(k)
    levels = np.array([10, -10, 5, -5, 0])
    a = np.random.permutation(np.resize(levels, k // 512 * 4)).reshape(k // 512, 4)
    idx = np.arange(k)
    return np.exp2(a[idx // 512, idx % 128 // 32])


BF16 = ml_dtypes.bfloat16


def bf(x):
    return np.asarray(x, np.float32).astype(BF16)


def f64(x):
    return np.asarray(x).astype(np.float64)


N, KS, C, ATT, MID = 4, 512, 1024, 128, 512


def setup_inputs():
    s = mx_kscale(C)
    a = 1.7 / ATT ** 0.25
    return {"x": bf(np.random.standard_normal((N, KS, C)) * s),
            "W_psi": bf(np.random.standard_normal((ATT, C)) / np.sqrt(C) / s),
            "b_psi": bf(np.random.standard_normal(ATT) * 0.3),
            "x_phi": bf(np.random.standard_normal((N, KS, ATT)) * a),
            "x_theta": bf(np.random.standard_normal((N, KS, ATT)) * a)}


def reference(x, W_psi, b_psi, x_phi, x_theta):
    x3 = (mxq(f64(x), 2, "e4m3") @ mxq(f64(W_psi), 1, "e4m3").T) + f64(b_psi)
    sc = f64(x_phi) @ f64(x_theta).transpose(0, 2, 1)
    e = np.exp(sc - sc.max(axis=1, keepdims=True))
    cov = e / e.sum(axis=1, keepdims=True)
    return mxq(cov, 2, "e4m3") @ mxq(x3, 1, "e4m3")

@@ -1,0 +1,183 @@
+import concourse.mybir as mybir
+from concourse.masks import make_identity
+
+F32 = mybir.dt.float32
+BF16 = mybir.dt.bfloat16
+U32 = mybir.dt.uint32
+U8 = mybir.dt.uint8
+FP8X4 = mybir.dt.float8_e4m3fn_x4
+
+P = 128
+PACK = 4
+SAMPLES = 4
+TOKENS = 512
+CHANNELS = 1024
+ATT = 128
+TILES = TOKENS // P
+PASSES = CHANNELS // (P * PACK)
+HALVES = 2
+
+FLOPS = 2 * SAMPLES * TOKENS * ATT * (CHANNELS + 2 * TOKENS)
+
+
+def tile_vc_interaction_sa_module_pa_kernel(tc, x, W_psi, b_psi, x_phi, x_theta, out):
+    nc = tc.nc
+    Exp = mybir.ActivationFunctionType.Exp
+
+    with tc.tile_pool(name="const", bufs=1) as const, tc.tile_pool(
+        name="loads", bufs=SAMPLES
+    ) as loads, tc.tile_pool(name="work", bufs=2) as work, tc.psum_pool(
+        name="psum_one", bufs=1
+    ) as psum_one, tc.psum_pool(name="psum_xt", bufs=2) as psum_xt, tc.psum_pool(
+        name="psum_sc", bufs=3
+    ) as psum_sc:
+        theta_in, phi_in, x_in = [], [], []
+        w_sb = const.tile([P, CHANNELS], BF16)
+        for n in range(SAMPLES):
+            theta_sb = loads.tile([P, TILES, ATT], BF16)
+            nc.sync.dma_start(out=theta_sb[:], in_=x_theta[n].rearrange("(p t) a -> p t a", t=TILES))
+            phi_sb = loads.tile([P, TILES, ATT], BF16)
+            nc.sync.dma_start(out=phi_sb[:], in_=x_phi[n].rearrange("(p t) a -> p t a", t=TILES))
+            if n == 0:
+                nc.sync.dma_start(out=w_sb[:], in_=W_psi)
+            x_sb = loads.tile([P, TILES, CHANNELS], BF16)
+            nc.sync.dma_start(out=x_sb[:], in_=x[n].rearrange("(p t) c -> p t c", t=TILES))
+            theta_in.append(theta_sb)
+            phi_in.append(phi_sb)
+            x_in.append(x_sb)
+        bias_bc = const.tile([P, ATT], BF16)
+        nc.gpsimd.dma_start(out=bias_bc[:], in_=b_psi.partition_broadcast(P))
+
+        ident_bf = const.tile([P, P], BF16)
+        make_identity(nc, ident_bf[:])
+        ident_f32 = const.tile([P, P], F32)
+        make_identity(nc, ident_f32[:])
+        warm_in = const.tile([P, 1], F32)
+        nc.vector.memset(warm_in[:], 0.0)
+        warm_out = const.tile([P, 1], F32)
+        nc.scalar.activation(out=warm_out[:], in_=warm_in[:], func=Exp)
+
+        def channels_to_partitions(rows_bf16, grouped_words):
+            words = rows_bf16.bitcast(F32)
+            turned = psum_xt.tile([P, PASSES, HALVES, P], F32)
+            for g in range(PASSES):
+                for u in range(HALVES):
+                    k = g * HALVES + u
+                    nc.tensor.transpose(out=turned[:, g, u, :], in_=words[:, k * P : (k + 1) * P], identity=ident_f32[:])
+            nc.scalar.copy(out=grouped_words, in_=turned[:].rearrange("q g u r -> q g r u"))
+
+        w_grouped = const.tile([P, PASSES, ATT, PACK], BF16, align_bytes=64)
+        channels_to_partitions(w_sb[:], w_grouped[:].bitcast(F32))
+        w_codes = const.tile([P, PASSES, ATT], U32, align_bytes=64)
+        w_scales = const.tile([P, PASSES, ATT], U8, align_bytes=64)
+        nc.vector.quantize_mx(
+            out=w_codes[:].rearrange("q g a -> q (g a)").bitcast(FP8X4),
+            scales=w_scales[:].rearrange("q g a -> q (g a)"),
+            in_=w_grouped[:].rearrange("q g a v -> q (g a v)"),
+        )
+
+        for n in range(SAMPLES):
+            turned_pt = psum_one.tile([P, 2 * TILES, P], BF16)
+            for t in range(TILES):
+                nc.tensor.transpose(out=turned_pt[:, t, :], in_=theta_in[n][:, t, :], identity=ident_bf[:])
+            for m in range(TILES):
+                nc.tensor.transpose(out=turned_pt[:, TILES + m, :], in_=phi_in[n][:, m, :], identity=ident_bf[:])
+            features = work.tile([P, 2 * TILES, P], BF16)
+            nc.scalar.copy(out=features[:], in_=turned_pt[:])
+
+            neg_max = work.tile([P, TILES], F32)
+            col_sum = work.tile([P, TILES], F32)
+            expo = work.tile([P, TILES, TOKENS], F32)
+            for t in range(TILES):
+                scores = psum_sc.tile([P, TOKENS], F32)
+                nc.tensor.matmul(
+                    out=scores[:],
+                    lhsT=features[:, t, :],
+                    rhs=features[:, TILES:, :].rearrange("a m r -> a (m r)"),
+                    start=True,
+                    stop=True,
+                )
+                nc.vector.tensor_reduce(
+                    out=neg_max[:, t : t + 1],
+                    in_=scores[:],
+                    axis=mybir.AxisListType.X,
+                    op=mybir.AluOpType.max,
+                    negate=True,
+                )
+                nc.scalar.activation(
+                    out=expo[:, t, :],
+                    in_=scores[:],
+                    func=Exp,
+                    bias=neg_max[:, t : t + 1],
+                    scale=1.0,
+                    accum_out=col_sum[:, t : t + 1],
+                )
+            inv_sum = work.tile([P, TILES], F32)
+            nc.vector.reciprocal(out=inv_sum[:], in_=col_sum[:])
+            cov_grouped = work.tile([P, TOKENS, PACK], BF16, align_bytes=64)
+            nc.vector.tensor_tensor(
+                out=cov_grouped[:],
+                in0=expo[:].rearrange("p t i -> p i t"),
+                in1=inv_sum[:].unsqueeze(1).to_broadcast([P, TOKENS, PACK]),
+                op=mybir.AluOpType.mult,
+            )
+            cov_codes = work.tile([P, TOKENS], U32, align_bytes=64)
+            cov_scales = work.tile([P, TOKENS], U8, align_bytes=64)
+            nc.vector.quantize_mx(
+                out=cov_codes[:].bitcast(FP8X4),
+                scales=cov_scales[:],
+                in_=cov_grouped[:].rearrange("p i t -> p (i t)"),
+            )
+
+            x_grouped = work.tile([P, TILES, PASSES, P, PACK], BF16, align_bytes=64)
+            x_grouped_words = x_grouped[:].bitcast(F32)
+            for t in range(TILES):
+                channels_to_partitions(x_in[n][:, t, :], x_grouped_words[:, t])
+            x_codes = work.tile([P, TILES, PASSES, P], U32, align_bytes=64)
+            x_scales = work.tile([P, TILES, PASSES, P], U8, align_bytes=64)
+            nc.vector.quantize_mx(
+                out=x_codes[:].rearrange("q t g r -> q (t g r)").bitcast(FP8X4),
+                scales=x_scales[:].rearrange("q t g r -> q (t g r)"),
+                in_=x_grouped[:].rearrange("q t g r v -> q (t g r v)"),
+            )
+            x3_acc = psum_one.tile([P, TILES, ATT], F32)
+            for t in range(TILES):
+                for g in range(PASSES):
+                    nc.tensor.matmul_mx(
+                        out=x3_acc[:, t, :],
+                        lhsT=x_codes[:, t, g, :].bitcast(FP8X4),
+                        lhsT_scale=x_scales[:, t, g, :],
+                        rhs=w_codes[:, g, :].bitcast(FP8X4),
+                        rhs_scale=w_scales[:, g, :],
+                        start=(g == 0),
+                        stop=(g == PASSES - 1),
+                    )
+            x3_grouped = work.tile([P, ATT, PACK], BF16, align_bytes=64)
+            nc.vector.tensor_tensor(
+                out=x3_grouped[:],
+                in0=x3_acc[:].rearrange("p t a -> p a t"),
+                in1=bias_bc[:].unsqueeze(2).to_broadcast([P, ATT, PACK]),
+                op=mybir.AluOpType.add,
+            )
+            x3_codes = work.tile([P, ATT], U32, align_bytes=64)
+            x3_scales = work.tile([P, ATT], U8, align_bytes=64)
+            nc.vector.quantize_mx(
+                out=x3_codes[:].bitcast(FP8X4),
+                scales=x3_scales[:],
+                in_=x3_grouped[:].rearrange("p a t -> p (a t)"),
+            )
+
+            out_acc = psum_one.tile([P, TILES, ATT], F32)
+            for m in range(TILES):
+                nc.tensor.matmul_mx(
+                    out=out_acc[:, m, :],
+                    lhsT=cov_codes[:, m * P : (m + 1) * P].bitcast(FP8X4),
+                    lhsT_scale=cov_scales[:, m * P : (m + 1) * P],
+                    rhs=x3_codes[:].bitcast(FP8X4),
+                    rhs_scale=x3_scales[:],
+                    start=True,
+                    stop=True,
+                )
+            out_sb = work.tile([P, TILES, ATT], F32)
+            nc.scalar.copy(out=out_sb[:], in_=out_acc[:])
+            nc.sync.dma_start(out=out[n].rearrange("(r m) a -> r m a", m=TILES), in_=out_sb[:])

@@ -16,6 +16,7 @@ ATT = 128
 TILES = TOKENS // P
 PASSES = CHANNELS // (P * PACK)
 HALVES = 2
+XT_BANKS = 2
 
 FLOPS = 2 * SAMPLES * TOKENS * ATT * (CHANNELS + 2 * TOKENS)
 
@@ -28,9 +29,9 @@ def tile_vc_interaction_sa_module_pa_kernel(tc, x, W_psi, b_psi, x_phi, x_theta,
         name="loads", bufs=SAMPLES
     ) as loads, tc.tile_pool(name="work", bufs=2) as work, tc.psum_pool(
         name="psum_one", bufs=1
-    ) as psum_one, tc.psum_pool(name="psum_xt", bufs=2) as psum_xt, tc.psum_pool(
-        name="psum_sc", bufs=3
-    ) as psum_sc:
+    ) as psum_one, tc.psum_pool(name="psum_xt", bufs=XT_BANKS) as psum_xt, tc.psum_pool(
+        name="psum_sc", bufs=TILES
+    ) as psum_sc, tc.manual_schedule():
         theta_in, phi_in, x_in = [], [], []
         w_sb = const.tile([P, CHANNELS], BF16)
         for n in range(SAMPLES):
@@ -45,29 +46,162 @@ def tile_vc_interaction_sa_module_pa_kernel(tc, x, W_psi, b_psi, x_phi, x_theta,
             theta_in.append(theta_sb)
             phi_in.append(phi_sb)
             x_in.append(x_sb)
-        bias_bc = const.tile([P, ATT], BF16)
-        nc.gpsimd.dma_start(out=bias_bc[:], in_=b_psi.partition_broadcast(P))
 
         ident_bf = const.tile([P, P], BF16)
-        make_identity(nc, ident_bf[:])
+        nc.vector.memset(ident_bf[:], 0.0)
+        make_identity(nc, ident_bf[:], nomemset=True)
         ident_f32 = const.tile([P, P], F32)
-        make_identity(nc, ident_f32[:])
+        nc.vector.tensor_copy(out=ident_f32[:], in_=ident_bf[:])
+        bias_bc = const.tile([P, ATT], BF16)
+        nc.gpsimd.dma_start(out=bias_bc[:], in_=b_psi.partition_broadcast(P))
         warm_in = const.tile([P, 1], F32)
         nc.vector.memset(warm_in[:], 0.0)
         warm_out = const.tile([P, 1], F32)
         nc.scalar.activation(out=warm_out[:], in_=warm_in[:], func=Exp)
 
-        def channels_to_partitions(rows_bf16, grouped_words):
+        features, scores, neg_max, col_sum, expo = {}, {}, {}, {}, {}
+        cov_codes, cov_scales, cov_grouped = {}, {}, {}
+        x_turned, x_grouped, x_codes, x_scales = {}, {}, {}, {}
+        x3_acc, x3_grouped, x3_codes, x3_scales = {}, {}, {}, {}
+
+        def turn_channels(rows_bf16):
             words = rows_bf16.bitcast(F32)
             turned = psum_xt.tile([P, PASSES, HALVES, P], F32)
             for g in range(PASSES):
                 for u in range(HALVES):
                     k = g * HALVES + u
                     nc.tensor.transpose(out=turned[:, g, u, :], in_=words[:, k * P : (k + 1) * P], identity=ident_f32[:])
+            return turned
+
+        def group_channels(turned, grouped_words):
             nc.scalar.copy(out=grouped_words, in_=turned[:].rearrange("q g u r -> q g r u"))
 
+        def turn_features(n):
+            turned_pt = psum_one.tile([P, 2 * TILES, P], BF16)
+            for t in range(TILES):
+                nc.tensor.transpose(out=turned_pt[:, t, :], in_=theta_in[n][:, t, :], identity=ident_bf[:])
+            for m in range(TILES):
+                nc.tensor.transpose(out=turned_pt[:, TILES + m, :], in_=phi_in[n][:, m, :], identity=ident_bf[:])
+            return turned_pt
+
+        def copy_features(n, turned_pt):
+            features[n] = work.tile([P, 2 * TILES, P], BF16, name="features")
+            nc.scalar.copy(out=features[n][:], in_=turned_pt[:])
+
+        def score_tiles(n):
+            for t in range(TILES):
+                scores[n, t] = psum_sc.tile([P, TOKENS], F32, name="scores")
+                nc.tensor.matmul(
+                    out=scores[n, t][:],
+                    lhsT=features[n][:, t, :],
+                    rhs=features[n][:, TILES:, :].rearrange("a m r -> a (m r)"),
+                    start=True,
+                    stop=True,
+                )
+
+        def exponentials(n):
+            neg_max[n] = work.tile([P, TILES], F32, name="neg_max")
+            col_sum[n] = work.tile([P, TILES], F32, name="col_sum")
+            expo[n] = work.tile([P, TILES, TOKENS], F32, name="expo")
+            for t in range(TILES):
+                nc.vector.tensor_reduce(
+                    out=neg_max[n][:, t : t + 1],
+                    in_=scores[n, t][:],
+                    axis=mybir.AxisListType.X,
+                    op=mybir.AluOpType.max,
+                    negate=True,
+                )
+                nc.scalar.activation(
+                    out=expo[n][:, t, :],
+                    in_=scores[n, t][:],
+                    func=Exp,
+                    bias=neg_max[n][:, t : t + 1],
+                    scale=1.0,
+                    accum_out=col_sum[n][:, t : t + 1],
+                )
+
+        def normalise(n):
+            inv_sum = work.tile([P, TILES], F32)
+            nc.vector.reciprocal(out=inv_sum[:], in_=col_sum[n][:])
+            cov_grouped[n] = work.tile([P, TOKENS, PACK], BF16, align_bytes=64, name="cov_grouped")
+            nc.vector.tensor_tensor(
+                out=cov_grouped[n][:],
+                in0=expo[n][:].rearrange("p t i -> p i t"),
+                in1=inv_sum[:].unsqueeze(1).to_broadcast([P, TOKENS, PACK]),
+                op=mybir.AluOpType.mult,
+            )
+
+        def quantise_cov(n):
+            cov_codes[n] = work.tile([P, TOKENS], U32, align_bytes=64, name="cov_codes")
+            cov_scales[n] = work.tile([P, TOKENS], U8, align_bytes=64, name="cov_scales")
+            nc.vector.quantize_mx(
+                out=cov_codes[n][:].bitcast(FP8X4),
+                scales=cov_scales[n][:],
+                in_=cov_grouped[n][:].rearrange("p i t -> p (i t)"),
+            )
+
+        def quantise_x(n):
+            x_codes[n] = work.tile([P, TILES, PASSES, P], U32, align_bytes=64, name="x_codes")
+            x_scales[n] = work.tile([P, TILES, PASSES, P], U8, align_bytes=64, name="x_scales")
+            for first in range(0, TILES, XT_BANKS):
+                pair = slice(first, first + XT_BANKS)
+                nc.vector.quantize_mx(
+                    out=x_codes[n][:, pair].rearrange("q t g r -> q (t g r)").bitcast(FP8X4),
+                    scales=x_scales[n][:, pair].rearrange("q t g r -> q (t g r)"),
+                    in_=x_grouped[n][:, pair].rearrange("q t g r v -> q (t g r v)"),
+                )
+
+        def project(n):
+            x3_acc[n] = psum_one.tile([P, TILES, ATT], F32, name="x3_acc", tag="acc")
+            for t in range(TILES):
+                for g in range(PASSES):
+                    nc.tensor.matmul_mx(
+                        out=x3_acc[n][:, t, :],
+                        lhsT=x_codes[n][:, t, g, :].bitcast(FP8X4),
+                        lhsT_scale=x_scales[n][:, t, g, :],
+                        rhs=w_codes[:, g, :].bitcast(FP8X4),
+                        rhs_scale=w_scales[:, g, :],
+                        start=(g == 0),
+                        stop=(g == PASSES - 1),
+                    )
+
+        def add_bias(n):
+            x3_grouped[n] = work.tile([P, ATT, PACK], BF16, align_bytes=64, name="x3_grouped")
+            nc.vector.tensor_tensor(
+                out=x3_grouped[n][:],
+                in0=x3_acc[n][:].rearrange("p t a -> p a t"),
+                in1=bias_bc[:].unsqueeze(2).to_broadcast([P, ATT, PACK]),
+                op=mybir.AluOpType.add,
+            )
+
+        def quantise_x3(n):
+            x3_codes[n] = work.tile([P, ATT], U32, align_bytes=64, name="x3_codes")
+            x3_scales[n] = work.tile([P, ATT], U8, align_bytes=64, name="x3_scales")
+            nc.vector.quantize_mx(
+                out=x3_codes[n][:].bitcast(FP8X4),
+                scales=x3_scales[n][:],
+                in_=x3_grouped[n][:].rearrange("p a t -> p (a t)"),
+            )
+
+        def combine_and_store(n):
+            out_acc = psum_one.tile([P, TILES, ATT], F32, tag="acc")
+            for m in range(TILES):
+                nc.tensor.matmul_mx(
+                    out=out_acc[:, m, :],
+                    lhsT=cov_codes[n][:, m * P : (m + 1) * P].bitcast(FP8X4),
+                    lhsT_scale=cov_scales[n][:, m * P : (m + 1) * P],
+                    rhs=x3_codes[n][:].bitcast(FP8X4),
+                    rhs_scale=x3_scales[n][:],
+                    start=True,
+                    stop=True,
+                )
+            out_sb = work.tile([P, TILES, ATT], F32)
+            nc.scalar.copy(out=out_sb[:], in_=out_acc[:])
+            nc.sync.dma_start(out=out[n].rearrange("(r m) a -> r m a", m=TILES), in_=out_sb[:])
+
+        copy_features(0, turn_features(0))
         w_grouped = const.tile([P, PASSES, ATT, PACK], BF16, align_bytes=64)
-        channels_to_partitions(w_sb[:], w_grouped[:].bitcast(F32))
+        group_channels(turn_channels(w_sb[:]), w_grouped[:].bitcast(F32))
         w_codes = const.tile([P, PASSES, ATT], U32, align_bytes=64)
         w_scales = const.tile([P, PASSES, ATT], U8, align_bytes=64)
         nc.vector.quantize_mx(
@@ -75,109 +209,33 @@ def tile_vc_interaction_sa_module_pa_kernel(tc, x, W_psi, b_psi, x_phi, x_theta,
             scales=w_scales[:].rearrange("q g a -> q (g a)"),
             in_=w_grouped[:].rearrange("q g a v -> q (g a v)"),
         )
+        score_tiles(0)
 
-        for n in range(SAMPLES):
-            turned_pt = psum_one.tile([P, 2 * TILES, P], BF16)
-            for t in range(TILES):
-                nc.tensor.transpose(out=turned_pt[:, t, :], in_=theta_in[n][:, t, :], identity=ident_bf[:])
-            for m in range(TILES):
-                nc.tensor.transpose(out=turned_pt[:, TILES + m, :], in_=phi_in[n][:, m, :], identity=ident_bf[:])
-            features = work.tile([P, 2 * TILES, P], BF16)
-            nc.scalar.copy(out=features[:], in_=turned_pt[:])
-
-            neg_max = work.tile([P, TILES], F32)
-            col_sum = work.tile([P, TILES], F32)
-            expo = work.tile([P, TILES, TOKENS], F32)
-            for t in range(TILES):
-                scores = psum_sc.tile([P, TOKENS], F32)
-                nc.tensor.matmul(
-                    out=scores[:],
-                    lhsT=features[:, t, :],
-                    rhs=features[:, TILES:, :].rearrange("a m r -> a (m r)"),
-                    start=True,
-                    stop=True,
-                )
-                nc.vector.tensor_reduce(
-                    out=neg_max[:, t : t + 1],
-                    in_=scores[:],
-                    axis=mybir.AxisListType.X,
-                    op=mybir.AluOpType.max,
-                    negate=True,
-                )
-                nc.scalar.activation(
-                    out=expo[:, t, :],
-                    in_=scores[:],
-                    func=Exp,
-                    bias=neg_max[:, t : t + 1],
-                    scale=1.0,
-                    accum_out=col_sum[:, t : t + 1],
-                )
-            inv_sum = work.tile([P, TILES], F32)
-            nc.vector.reciprocal(out=inv_sum[:], in_=col_sum[:])
-            cov_grouped = work.tile([P, TOKENS, PACK], BF16, align_bytes=64)
-            nc.vector.tensor_tensor(
-                out=cov_grouped[:],
-                in0=expo[:].rearrange("p t i -> p i t"),
-                in1=inv_sum[:].unsqueeze(1).to_broadcast([P, TOKENS, PACK]),
-                op=mybir.AluOpType.mult,
-            )
-            cov_codes = work.tile([P, TOKENS], U32, align_bytes=64)
-            cov_scales = work.tile([P, TOKENS], U8, align_bytes=64)
-            nc.vector.quantize_mx(
-                out=cov_codes[:].bitcast(FP8X4),
-                scales=cov_scales[:],
-                in_=cov_grouped[:].rearrange("p i t -> p (i t)"),
-            )
-
-            x_grouped = work.tile([P, TILES, PASSES, P, PACK], BF16, align_bytes=64)
-            x_grouped_words = x_grouped[:].bitcast(F32)
-            for t in range(TILES):
-                channels_to_partitions(x_in[n][:, t, :], x_grouped_words[:, t])
-            x_codes = work.tile([P, TILES, PASSES, P], U32, align_bytes=64)
-            x_scales = work.tile([P, TILES, PASSES, P], U8, align_bytes=64)
-            nc.vector.quantize_mx(
-                out=x_codes[:].rearrange("q t g r -> q (t g r)").bitcast(FP8X4),
-                scales=x_scales[:].rearrange("q t g r -> q (t g r)"),
-                in_=x_grouped[:].rearrange("q t g r v -> q (t g r v)"),
-            )
-            x3_acc = psum_one.tile([P, TILES, ATT], F32)
-            for t in range(TILES):
-                for g in range(PASSES):
-                    nc.tensor.matmul_mx(
-                        out=x3_acc[:, t, :],
-                        lhsT=x_codes[:, t, g, :].bitcast(FP8X4),
-                        lhsT_scale=x_scales[:, t, g, :],
-                        rhs=w_codes[:, g, :].bitcast(FP8X4),
-                        rhs_scale=w_scales[:, g, :],
-                        start=(g == 0),
-                        stop=(g == PASSES - 1),
-                    )
-            x3_grouped = work.tile([P, ATT, PACK], BF16, align_bytes=64)
-            nc.vector.tensor_tensor(
-                out=x3_grouped[:],
-                in0=x3_acc[:].rearrange("p t a -> p a t"),
-                in1=bias_bc[:].unsqueeze(2).to_broadcast([P, ATT, PACK]),
-                op=mybir.AluOpType.add,
-            )
-            x3_codes = work.tile([P, ATT], U32, align_bytes=64)
-            x3_scales = work.tile([P, ATT], U8, align_bytes=64)
-            nc.vector.quantize_mx(
-                out=x3_codes[:].bitcast(FP8X4),
-                scales=x3_scales[:],
-                in_=x3_grouped[:].rearrange("p a t -> p (a t)"),
-            )
-
-            out_acc = psum_one.tile([P, TILES, ATT], F32)
-            for m in range(TILES):
-                nc.tensor.matmul_mx(
-                    out=out_acc[:, m, :],
-                    lhsT=cov_codes[:, m * P : (m + 1) * P].bitcast(FP8X4),
-                    lhsT_scale=cov_scales[:, m * P : (m + 1) * P],
-                    rhs=x3_codes[:].bitcast(FP8X4),
-                    rhs_scale=x3_scales[:],
-                    start=True,
-                    stop=True,
-                )
-            out_sb = work.tile([P, TILES, ATT], F32)
-            nc.scalar.copy(out=out_sb[:], in_=out_acc[:])
-            nc.sync.dma_start(out=out[n].rearrange("(r m) a -> r m a", m=TILES), in_=out_sb[:])
+        for n in range(-1, SAMPLES):
+            if n >= 0:
+                normalise(n)
+                quantise_x(n)
+                project(n)
+            if n + 2 < SAMPLES:
+                turned_pt = turn_features(n + 2)
+            if n + 1 < SAMPLES:
+                for t in range(XT_BANKS):
+                    x_turned[t] = turn_channels(x_in[n + 1][:, t, :])
+                exponentials(n + 1)
+            if n >= 0:
+                add_bias(n)
+                quantise_cov(n)
+                quantise_x3(n)
+            if n + 2 < SAMPLES:
+                copy_features(n + 2, turned_pt)
+            if n + 1 < SAMPLES:
+                x_grouped[n + 1] = work.tile([P, TILES, PASSES, P, PACK], BF16, align_bytes=64, name="x_grouped")
+                x_grouped_words = x_grouped[n + 1][:].bitcast(F32)
+                for t in range(TILES):
+                    group_channels(x_turned[t], x_grouped_words[:, t])
+                    if t + XT_BANKS < TILES:
+                        x_turned[t + XT_BANKS] = turn_channels(x_in[n + 1][:, t + XT_BANKS, :])
+            if n >= 0:
+                combine_and_store(n)
+            if n + 2 < SAMPLES:
+                score_tiles(n + 2)

@@ -17,6 +17,7 @@ TILES = TOKENS // P
 PASSES = CHANNELS // (P * PACK)
 HALVES = 2
 XT_BANKS = 2
+GPSIMD_STEP = 128
 
 FLOPS = 2 * SAMPLES * TOKENS * ATT * (CHANNELS + 2 * TOKENS)
 
@@ -42,7 +43,10 @@ def tile_vc_interaction_sa_module_pa_kernel(tc, x, W_psi, b_psi, x_phi, x_theta,
             if n == 0:
                 nc.sync.dma_start(out=w_sb[:], in_=W_psi)
             x_sb = loads.tile([P, TILES, CHANNELS], BF16)
-            nc.sync.dma_start(out=x_sb[:], in_=x[n].rearrange("(p t) c -> p t c", t=TILES))
+            x_rows = x[n].rearrange("(p t) c -> p t c", t=TILES)
+            step = TILES // 2 if n == 0 else TILES
+            for first in range(0, TILES, step):
+                nc.sync.dma_start(out=x_sb[:, first : first + step, :], in_=x_rows[:, first : first + step, :])
             theta_in.append(theta_sb)
             phi_in.append(phi_sb)
             x_in.append(x_sb)
@@ -60,28 +64,38 @@ def tile_vc_interaction_sa_module_pa_kernel(tc, x, W_psi, b_psi, x_phi, x_theta,
         nc.scalar.activation(out=warm_out[:], in_=warm_in[:], func=Exp)
 
         features, scores, neg_max, col_sum, expo = {}, {}, {}, {}, {}
-        cov_codes, cov_scales, cov_grouped = {}, {}, {}
+        cov_grouped, cov_codes, cov_scales = {}, {}, {}
         x_turned, x_grouped, x_codes, x_scales = {}, {}, {}, {}
         x3_acc, x3_grouped, x3_codes, x3_scales = {}, {}, {}, {}
 
         def turn_channels(rows_bf16):
             words = rows_bf16.bitcast(F32)
-            turned = psum_xt.tile([P, PASSES, HALVES, P], F32)
+            turned = psum_xt.tile([P, PASSES, HALVES, P], F32, name="turned", tag="turned")
             for g in range(PASSES):
                 for u in range(HALVES):
                     k = g * HALVES + u
                     nc.tensor.transpose(out=turned[:, g, u, :], in_=words[:, k * P : (k + 1) * P], identity=ident_f32[:])
             return turned
 
-        def group_channels(turned, grouped_words):
-            nc.scalar.copy(out=grouped_words, in_=turned[:].rearrange("q g u r -> q g r u"))
+        def group_channels(copy, turned, grouped_words):
+            copy(out=grouped_words, in_=turned[:].rearrange("q g u r -> q g r u"))
+
+        def turn_x(n, t):
+            x_turned[n, t] = turn_channels(x_in[n][:, t, :])
+
+        def group_x(copy, n, t):
+            if n not in x_grouped:
+                x_grouped[n] = work.tile([P, TILES, PASSES, P, PACK], BF16, align_bytes=64, name="x_grouped")
+            group_channels(copy, x_turned[n, t], x_grouped[n][:].bitcast(F32)[:, t])
+
+        def turn_tokens(rows, turned):
+            for t in range(TILES):
+                nc.tensor.transpose(out=turned[:, t, :], in_=rows[:, t, :], identity=ident_bf[:])
 
         def turn_features(n):
-            turned_pt = psum_one.tile([P, 2 * TILES, P], BF16)
-            for t in range(TILES):
-                nc.tensor.transpose(out=turned_pt[:, t, :], in_=theta_in[n][:, t, :], identity=ident_bf[:])
-            for m in range(TILES):
-                nc.tensor.transpose(out=turned_pt[:, TILES + m, :], in_=phi_in[n][:, m, :], identity=ident_bf[:])
+            turned_pt = psum_one.tile([P, 2 * TILES, P], BF16, name="turned_pt", tag="turned_pt")
+            turn_tokens(theta_in[n], turned_pt[:, :TILES, :])
+            turn_tokens(phi_in[n], turned_pt[:, TILES:, :])
             return turned_pt
 
         def copy_features(n, turned_pt):
@@ -120,14 +134,21 @@ def tile_vc_interaction_sa_module_pa_kernel(tc, x, W_psi, b_psi, x_phi, x_theta,
                     accum_out=col_sum[n][:, t : t + 1],
                 )
 
-        def normalise(n):
-            inv_sum = work.tile([P, TILES], F32)
+        def invert_sums(n, reader):
+            inv_sum = work.tile([P, TILES], F32, name="inv_sum_" + reader)
             nc.vector.reciprocal(out=inv_sum[:], in_=col_sum[n][:])
-            cov_grouped[n] = work.tile([P, TOKENS, PACK], BF16, align_bytes=64, name="cov_grouped")
-            nc.vector.tensor_tensor(
-                out=cov_grouped[n][:],
-                in0=expo[n][:].rearrange("p t i -> p i t"),
-                in1=inv_sum[:].unsqueeze(1).to_broadcast([P, TOKENS, PACK]),
+            return inv_sum
+
+        def vector_rows(n):
+            return TOKENS
+
+        def normalise(engine, n, inv_sum, rows):
+            if n not in cov_grouped:
+                cov_grouped[n] = work.tile([P, TOKENS, PACK], BF16, align_bytes=64, name="cov_grouped")
+            engine.tensor_tensor(
+                out=cov_grouped[n][:, rows, :],
+                in0=expo[n][:, :, rows].rearrange("p t i -> p i t"),
+                in1=inv_sum[:].unsqueeze(1).to_broadcast([P, rows.stop - rows.start, PACK]),
                 op=mybir.AluOpType.mult,
             )
 
@@ -184,7 +205,7 @@ def tile_vc_interaction_sa_module_pa_kernel(tc, x, W_psi, b_psi, x_phi, x_theta,
             )
 
         def combine_and_store(n):
-            out_acc = psum_one.tile([P, TILES, ATT], F32, tag="acc")
+            out_acc = psum_one.tile([P, TILES, ATT], F32, name="out_acc", tag="acc")
             for m in range(TILES):
                 nc.tensor.matmul_mx(
                     out=out_acc[:, m, :],
@@ -199,9 +220,18 @@ def tile_vc_interaction_sa_module_pa_kernel(tc, x, W_psi, b_psi, x_phi, x_theta,
             nc.scalar.copy(out=out_sb[:], in_=out_acc[:])
             nc.sync.dma_start(out=out[n].rearrange("(r m) a -> r m a", m=TILES), in_=out_sb[:])
 
-        copy_features(0, turn_features(0))
+        features[0] = work.tile([P, 2 * TILES, P], BF16, name="features")
+        theta_turned = psum_one.tile([P, 2 * TILES, P], BF16, name="turned_pt", tag="turned_pt")
+        phi_turned = psum_xt.tile([P, TILES, P], BF16, name="phi_turned", tag="turned")
+        turn_tokens(theta_in[0], theta_turned[:, :TILES, :])
+        nc.scalar.copy(out=features[0][:, :TILES, :], in_=theta_turned[:, :TILES, :])
+        turn_tokens(phi_in[0], phi_turned[:])
+        nc.vector.tensor_copy(out=features[0][:, TILES:, :], in_=phi_turned[:])
+        w_turned = turn_channels(w_sb[:])
+        score_tiles(0)
         w_grouped = const.tile([P, PASSES, ATT, PACK], BF16, align_bytes=64)
-        group_channels(turn_channels(w_sb[:]), w_grouped[:].bitcast(F32))
+        group_channels(nc.scalar.copy, w_turned, w_grouped[:].bitcast(F32))
+        exponentials(0)
         w_codes = const.tile([P, PASSES, ATT], U32, align_bytes=64)
         w_scales = const.tile([P, PASSES, ATT], U8, align_bytes=64)
         nc.vector.quantize_mx(
@@ -209,33 +239,44 @@ def tile_vc_interaction_sa_module_pa_kernel(tc, x, W_psi, b_psi, x_phi, x_theta,
             scales=w_scales[:].rearrange("q g a -> q (g a)"),
             in_=w_grouped[:].rearrange("q g a v -> q (g a v)"),
         )
-        score_tiles(0)
+        for t in range(XT_BANKS):
+            turn_x(0, t)
+        turned_pt = turn_features(1)
+        copy_features(1, turned_pt)
+        for t in range(XT_BANKS):
+            group_x(nc.vector.tensor_copy, 0, t)
+            turn_x(0, t + XT_BANKS)
+        score_tiles(1)
+        for t in range(XT_BANKS, TILES):
+            group_x(nc.scalar.copy, 0, t)
 
-        for n in range(-1, SAMPLES):
-            if n >= 0:
-                normalise(n)
-                quantise_x(n)
-                project(n)
+        for n in range(SAMPLES):
+            inv_vector = invert_sums(n, "vector")
+            if n > 0:
+                quantise_x3(n - 1)
+                combine_and_store(n - 1)
+            normalise(nc.vector, n, inv_vector, slice(0, vector_rows(n)))
+            if vector_rows(n) < TOKENS:
+                inv_gpsimd = invert_sums(n, "gpsimd")
+                for first in range(vector_rows(n), TOKENS, GPSIMD_STEP):
+                    normalise(nc.gpsimd, n, inv_gpsimd, slice(first, first + GPSIMD_STEP))
             if n + 2 < SAMPLES:
                 turned_pt = turn_features(n + 2)
             if n + 1 < SAMPLES:
                 for t in range(XT_BANKS):
-                    x_turned[t] = turn_channels(x_in[n + 1][:, t, :])
+                    turn_x(n + 1, t)
                 exponentials(n + 1)
-            if n >= 0:
-                add_bias(n)
-                quantise_cov(n)
-                quantise_x3(n)
+            quantise_x(n)
+            project(n)
+            quantise_cov(n)
+            add_bias(n)
             if n + 2 < SAMPLES:
                 copy_features(n + 2, turned_pt)
-            if n + 1 < SAMPLES:
-                x_grouped[n + 1] = work.tile([P, TILES, PASSES, P, PACK], BF16, align_bytes=64, name="x_grouped")
-                x_grouped_words = x_grouped[n + 1][:].bitcast(F32)
-                for t in range(TILES):
-                    group_channels(x_turned[t], x_grouped_words[:, t])
-                    if t + XT_BANKS < TILES:
-                        x_turned[t + XT_BANKS] = turn_channels(x_in[n + 1][:, t + XT_BANKS, :])
-            if n >= 0:
-                combine_and_store(n)
-            if n + 2 < SAMPLES:
                 score_tiles(n + 2)
+            if n + 1 < SAMPLES:
+                for t in range(TILES):
+                    group_x(nc.scalar.copy, n + 1, t)
+                    if t + XT_BANKS < TILES:
+                        turn_x(n + 1, t + XT_BANKS)
+        quantise_x3(SAMPLES - 1)
+        combine_and_store(SAMPLES - 1)

@@ -18,6 +18,7 @@ PASSES = CHANNELS // (P * PACK)
 HALVES = 2
 XT_BANKS = 2
 GPSIMD_STEP = 128
+RUN = 4
 
 FLOPS = 2 * SAMPLES * TOKENS * ATT * (CHANNELS + 2 * TOKENS)
 
@@ -146,9 +147,9 @@ def tile_vc_interaction_sa_module_pa_kernel(tc, x, W_psi, b_psi, x_phi, x_theta,
             if n not in cov_grouped:
                 cov_grouped[n] = work.tile([P, TOKENS, PACK], BF16, align_bytes=64, name="cov_grouped")
             engine.tensor_tensor(
-                out=cov_grouped[n][:, rows, :],
-                in0=expo[n][:, :, rows].rearrange("p t i -> p i t"),
-                in1=inv_sum[:].unsqueeze(1).to_broadcast([P, rows.stop - rows.start, PACK]),
+                out=cov_grouped[n][:, rows, :].rearrange("p (c i) t -> p c t i", i=RUN),
+                in0=expo[n][:, :, rows].rearrange("p t (c i) -> p c t i", i=RUN),
+                in1=inv_sum[:].unsqueeze(1).unsqueeze(3).to_broadcast([P, (rows.stop - rows.start) // RUN, PACK, RUN]),
                 op=mybir.AluOpType.mult,
             )
 

@@ -141,7 +141,7 @@ def tile_vc_interaction_sa_module_pa_kernel(tc, x, W_psi, b_psi, x_phi, x_theta,
             return inv_sum
 
         def vector_rows(n):
-            return TOKENS
+            return TOKENS // 2 if n + 1 < SAMPLES else TOKENS
 
         def normalise(engine, n, inv_sum, rows):
             if n not in cov_grouped:

@@ -37,11 +37,11 @@ def tile_vc_interaction_sa_module_pa_kernel(tc, x, W_psi, b_psi, x_phi, x_theta,
         theta_in, phi_in, x_in = [], [], []
         w_sb = const.tile([P, CHANNELS], BF16)
         for n in range(SAMPLES):
-            theta_sb = loads.tile([P, TILES, ATT], BF16)
-            nc.sync.dma_start(out=theta_sb[:], in_=x_theta[n].rearrange("(p t) a -> p t a", t=TILES))
             phi_sb = loads.tile([P, TILES, ATT], BF16)
             nc.sync.dma_start(out=phi_sb[:], in_=x_phi[n].rearrange("(p t) a -> p t a", t=TILES))
-            if n == 0:
+            theta_sb = loads.tile([P, TILES, ATT], BF16)
+            nc.sync.dma_start(out=theta_sb[:], in_=x_theta[n].rearrange("(p t) a -> p t a", t=TILES))
+            if n == 1:
                 nc.sync.dma_start(out=w_sb[:], in_=W_psi)
             x_sb = loads.tile([P, TILES, CHANNELS], BF16)
             x_rows = x[n].rearrange("(p t) c -> p t c", t=TILES)
@@ -90,13 +90,13 @@ def tile_vc_interaction_sa_module_pa_kernel(tc, x, W_psi, b_psi, x_phi, x_theta,
             group_channels(copy, x_turned[n, t], x_grouped[n][:].bitcast(F32)[:, t])
 
         def turn_tokens(rows, turned):
-            for t in range(TILES):
+            for t in range(rows.shape[1]):
                 nc.tensor.transpose(out=turned[:, t, :], in_=rows[:, t, :], identity=ident_bf[:])
 
         def turn_features(n):
             turned_pt = psum_one.tile([P, 2 * TILES, P], BF16, name="turned_pt", tag="turned_pt")
-            turn_tokens(theta_in[n], turned_pt[:, :TILES, :])
-            turn_tokens(phi_in[n], turned_pt[:, TILES:, :])
+            turn_tokens(theta_in[n][:], turned_pt[:, :TILES, :])
+            turn_tokens(phi_in[n][:], turned_pt[:, TILES:, :])
             return turned_pt
 
         def copy_features(n, turned_pt):
@@ -140,9 +140,6 @@ def tile_vc_interaction_sa_module_pa_kernel(tc, x, W_psi, b_psi, x_phi, x_theta,
             nc.vector.reciprocal(out=inv_sum[:], in_=col_sum[n][:])
             return inv_sum
 
-        def vector_rows(n):
-            return TOKENS // 2 if n + 1 < SAMPLES else TOKENS
-
         def normalise(engine, n, inv_sum, rows):
             if n not in cov_grouped:
                 cov_grouped[n] = work.tile([P, TOKENS, PACK], BF16, align_bytes=64, name="cov_grouped")
@@ -153,13 +150,14 @@ def tile_vc_interaction_sa_module_pa_kernel(tc, x, W_psi, b_psi, x_phi, x_theta,
                 op=mybir.AluOpType.mult,
             )
 
-        def quantise_cov(n):
-            cov_codes[n] = work.tile([P, TOKENS], U32, align_bytes=64, name="cov_codes")
-            cov_scales[n] = work.tile([P, TOKENS], U8, align_bytes=64, name="cov_scales")
+        def quantise_cov(n, rows):
+            if n not in cov_codes:
+                cov_codes[n] = work.tile([P, TOKENS], U32, align_bytes=64, name="cov_codes")
+                cov_scales[n] = work.tile([P, TOKENS], U8, align_bytes=64, name="cov_scales")
             nc.vector.quantize_mx(
-                out=cov_codes[n][:].bitcast(FP8X4),
-                scales=cov_scales[n][:],
-                in_=cov_grouped[n][:].rearrange("p i t -> p (i t)"),
+                out=cov_codes[n][:, rows].bitcast(FP8X4),
+                scales=cov_scales[n][:, rows],
+                in_=cov_grouped[n][:, rows, :].rearrange("p i t -> p (i t)"),
             )
 
         def quantise_x(n):
@@ -205,11 +203,10 @@ def tile_vc_interaction_sa_module_pa_kernel(tc, x, W_psi, b_psi, x_phi, x_theta,
                 in_=x3_grouped[n][:].rearrange("p a t -> p (a t)"),
             )
 
-        def combine_and_store(n):
-            out_acc = psum_one.tile([P, TILES, ATT], F32, name="out_acc", tag="acc")
-            for m in range(TILES):
+        def combine_and_store(n, tiles, out_acc, copy):
+            for m in tiles:
                 nc.tensor.matmul_mx(
-                    out=out_acc[:, m, :],
+                    out=out_acc[:, m - tiles.start, :],
                     lhsT=cov_codes[n][:, m * P : (m + 1) * P].bitcast(FP8X4),
                     lhsT_scale=cov_scales[n][:, m * P : (m + 1) * P],
                     rhs=x3_codes[n][:].bitcast(FP8X4),
@@ -217,67 +214,91 @@ def tile_vc_interaction_sa_module_pa_kernel(tc, x, W_psi, b_psi, x_phi, x_theta,
                     start=True,
                     stop=True,
                 )
-            out_sb = work.tile([P, TILES, ATT], F32)
-            nc.scalar.copy(out=out_sb[:], in_=out_acc[:])
-            nc.sync.dma_start(out=out[n].rearrange("(r m) a -> r m a", m=TILES), in_=out_sb[:])
+            out_sb = work.tile([P, len(tiles), ATT], F32, name="out_sb")
+            copy(out=out_sb[:], in_=out_acc[:])
+            out_rows = out[n].rearrange("(r m) a -> r m a", m=TILES)
+            nc.sync.dma_start(out=out_rows[:, tiles.start : tiles.stop, :], in_=out_sb[:])
 
         features[0] = work.tile([P, 2 * TILES, P], BF16, name="features")
-        theta_turned = psum_one.tile([P, 2 * TILES, P], BF16, name="turned_pt", tag="turned_pt")
         phi_turned = psum_xt.tile([P, TILES, P], BF16, name="phi_turned", tag="turned")
-        turn_tokens(theta_in[0], theta_turned[:, :TILES, :])
-        nc.scalar.copy(out=features[0][:, :TILES, :], in_=theta_turned[:, :TILES, :])
-        turn_tokens(phi_in[0], phi_turned[:])
+        first_turned = psum_xt.tile([P, 1, P], BF16, name="first_turned", tag="turned")
+        rest_turned = psum_one.tile([P, TILES - 1, P], BF16, name="rest_turned", tag="turned_pt")
+        turn_tokens(phi_in[0][:], phi_turned[:])
         nc.vector.tensor_copy(out=features[0][:, TILES:, :], in_=phi_turned[:])
-        w_turned = turn_channels(w_sb[:])
+        turn_tokens(theta_in[0][:, :1, :], first_turned[:])
+        nc.scalar.copy(out=features[0][:, :1, :], in_=first_turned[:])
+        turn_tokens(theta_in[0][:, 1:, :], rest_turned[:])
+        nc.scalar.copy(out=features[0][:, 1:TILES, :], in_=rest_turned[:])
         score_tiles(0)
-        w_grouped = const.tile([P, PASSES, ATT, PACK], BF16, align_bytes=64)
-        group_channels(nc.scalar.copy, w_turned, w_grouped[:].bitcast(F32))
         exponentials(0)
-        w_codes = const.tile([P, PASSES, ATT], U32, align_bytes=64)
-        w_scales = const.tile([P, PASSES, ATT], U8, align_bytes=64)
-        nc.vector.quantize_mx(
-            out=w_codes[:].rearrange("q g a -> q (g a)").bitcast(FP8X4),
-            scales=w_scales[:].rearrange("q g a -> q (g a)"),
-            in_=w_grouped[:].rearrange("q g a v -> q (g a v)"),
-        )
         for t in range(XT_BANKS):
             turn_x(0, t)
         turned_pt = turn_features(1)
         copy_features(1, turned_pt)
-        for t in range(XT_BANKS):
-            group_x(nc.vector.tensor_copy, 0, t)
-            turn_x(0, t + XT_BANKS)
+        group_x(nc.vector.tensor_copy, 0, 0)
+        w_turned = turn_channels(w_sb[:])
         score_tiles(1)
+        w_grouped = const.tile([P, PASSES, ATT, PACK], BF16, align_bytes=64)
+        group_channels(nc.scalar.copy, w_turned, w_grouped[:].bitcast(F32))
+        group_x(nc.vector.tensor_copy, 0, 1)
         for t in range(XT_BANKS, TILES):
+            turn_x(0, t)
             group_x(nc.scalar.copy, 0, t)
+        w_codes = const.tile([P, PASSES, ATT], U32, align_bytes=64)
+        w_scales = const.tile([P, PASSES, ATT], U8, align_bytes=64)
 
-        for n in range(SAMPLES):
+        def quantise_w():
+            nc.vector.quantize_mx(
+                out=w_codes[:].rearrange("q g a -> q (g a)").bitcast(FP8X4),
+                scales=w_scales[:].rearrange("q g a -> q (g a)"),
+                in_=w_grouped[:].rearrange("q g a v -> q (g a v)"),
+            )
+
+        everything = slice(0, TOKENS)
+        first_half, second_half = slice(0, TOKENS // 2), slice(TOKENS // 2, TOKENS)
+        for n in range(SAMPLES - 1):
             inv_vector = invert_sums(n, "vector")
             if n > 0:
                 quantise_x3(n - 1)
-                combine_and_store(n - 1)
-            normalise(nc.vector, n, inv_vector, slice(0, vector_rows(n)))
-            if vector_rows(n) < TOKENS:
-                inv_gpsimd = invert_sums(n, "gpsimd")
-                for first in range(vector_rows(n), TOKENS, GPSIMD_STEP):
-                    normalise(nc.gpsimd, n, inv_gpsimd, slice(first, first + GPSIMD_STEP))
+                out_acc = psum_one.tile([P, TILES, ATT], F32, name="out_acc", tag="acc")
+                combine_and_store(n - 1, range(TILES), out_acc, nc.scalar.copy)
+            normalise(nc.vector, n, inv_vector, first_half)
+            inv_gpsimd = invert_sums(n, "gpsimd")
+            for first in range(second_half.start, second_half.stop, GPSIMD_STEP):
+                normalise(nc.gpsimd, n, inv_gpsimd, slice(first, first + GPSIMD_STEP))
             if n + 2 < SAMPLES:
                 turned_pt = turn_features(n + 2)
-            if n + 1 < SAMPLES:
-                for t in range(XT_BANKS):
-                    turn_x(n + 1, t)
-                exponentials(n + 1)
+            for t in range(XT_BANKS):
+                turn_x(n + 1, t)
+            exponentials(n + 1)
+            if n == 0:
+                quantise_w()
             quantise_x(n)
             project(n)
-            quantise_cov(n)
+            quantise_cov(n, everything)
             add_bias(n)
             if n + 2 < SAMPLES:
                 copy_features(n + 2, turned_pt)
                 score_tiles(n + 2)
-            if n + 1 < SAMPLES:
-                for t in range(TILES):
-                    group_x(nc.scalar.copy, n + 1, t)
-                    if t + XT_BANKS < TILES:
-                        turn_x(n + 1, t + XT_BANKS)
-        quantise_x3(SAMPLES - 1)
-        combine_and_store(SAMPLES - 1)
+            for t in range(TILES):
+                group_x(nc.scalar.copy, n + 1, t)
+                if t + XT_BANKS < TILES:
+                    turn_x(n + 1, t + XT_BANKS)
+
+        n = SAMPLES - 1
+        inv_vector = invert_sums(n, "vector")
+        quantise_x3(n - 1)
+        out_acc = psum_one.tile([P, TILES, ATT], F32, name="out_acc", tag="acc")
+        combine_and_store(n - 1, range(TILES), out_acc, nc.scalar.copy)
+        normalise(nc.vector, n, inv_vector, first_half)
+        quantise_x(n)
+        project(n)
+        normalise(nc.vector, n, inv_vector, second_half)
+        add_bias(n)
+        quantise_cov(n, first_half)
+        quantise_x3(n)
+        quantise_cov(n, second_half)
+        for half, copy in ((0, nc.scalar.copy), (1, nc.vector.tensor_copy)):
+            tiles = range(half * TILES // 2, (half + 1) * TILES // 2)
+            half_acc = psum_xt.tile([P, TILES // 2, ATT], F32, name="half_acc", tag="turned")
+            combine_and_store(n, tiles, half_acc, copy)

@@ -36,6 +36,7 @@ def tile_vc_interaction_sa_module_pa_kernel(tc, x, W_psi, b_psi, x_phi, x_theta,
     ) as psum_sc, tc.manual_schedule():
         theta_in, phi_in, x_in = [], [], []
         w_sb = const.tile([P, CHANNELS], BF16)
+        bias_bc = const.tile([P, ATT], BF16)
         for n in range(SAMPLES):
             phi_sb = loads.tile([P, TILES, ATT], BF16)
             nc.sync.dma_start(out=phi_sb[:], in_=x_phi[n].rearrange("(p t) a -> p t a", t=TILES))
@@ -43,6 +44,7 @@ def tile_vc_interaction_sa_module_pa_kernel(tc, x, W_psi, b_psi, x_phi, x_theta,
             nc.sync.dma_start(out=theta_sb[:], in_=x_theta[n].rearrange("(p t) a -> p t a", t=TILES))
             if n == 1:
                 nc.sync.dma_start(out=w_sb[:], in_=W_psi)
+                nc.sync.dma_start(out=bias_bc[:], in_=b_psi.partition_broadcast(P))
             x_sb = loads.tile([P, TILES, CHANNELS], BF16)
             x_rows = x[n].rearrange("(p t) c -> p t c", t=TILES)
             step = TILES // 2 if n == 0 else TILES
@@ -57,8 +59,6 @@ def tile_vc_interaction_sa_module_pa_kernel(tc, x, W_psi, b_psi, x_phi, x_theta,
         make_identity(nc, ident_bf[:], nomemset=True)
         ident_f32 = const.tile([P, P], F32)
         nc.vector.tensor_copy(out=ident_f32[:], in_=ident_bf[:])
-        bias_bc = const.tile([P, ATT], BF16)
-        nc.gpsimd.dma_start(out=bias_bc[:], in_=b_psi.partition_broadcast(P))
         warm_in = const.tile([P, 1], F32)
         nc.vector.memset(warm_in[:], 0.0)
         warm_out = const.tile([P, 1], F32)

@@ -18,7 +18,7 @@ PASSES = CHANNELS // (P * PACK)
 HALVES = 2
 XT_BANKS = 2
 GPSIMD_STEP = 128
-RUN = 4
+RUN = 2
 
 FLOPS = 2 * SAMPLES * TOKENS * ATT * (CHANNELS + 2 * TOKENS)
 

@@ -17,7 +17,8 @@ TILES = TOKENS // P
 PASSES = CHANNELS // (P * PACK)
 HALVES = 2
 XT_BANKS = 2
-GPSIMD_STEP = 128
+VECTOR_ROWS = 320
+GPSIMD_STEP = 64
 RUN = 2
 
 FLOPS = 2 * SAMPLES * TOKENS * ATT * (CHANNELS + 2 * TOKENS)
@@ -256,15 +257,16 @@ def tile_vc_interaction_sa_module_pa_kernel(tc, x, W_psi, b_psi, x_phi, x_theta,
 
         everything = slice(0, TOKENS)
         first_half, second_half = slice(0, TOKENS // 2), slice(TOKENS // 2, TOKENS)
+        vector_share, gpsimd_share = slice(0, VECTOR_ROWS), slice(VECTOR_ROWS, TOKENS)
         for n in range(SAMPLES - 1):
             inv_vector = invert_sums(n, "vector")
             if n > 0:
                 quantise_x3(n - 1)
                 out_acc = psum_one.tile([P, TILES, ATT], F32, name="out_acc", tag="acc")
                 combine_and_store(n - 1, range(TILES), out_acc, nc.scalar.copy)
-            normalise(nc.vector, n, inv_vector, first_half)
+            normalise(nc.vector, n, inv_vector, vector_share)
             inv_gpsimd = invert_sums(n, "gpsimd")
-            for first in range(second_half.start, second_half.stop, GPSIMD_STEP):
+            for first in range(gpsimd_share.start, gpsimd_share.stop, GPSIMD_STEP):
                 normalise(nc.gpsimd, n, inv_gpsimd, slice(first, first + GPSIMD_STEP))
             if n + 2 < SAMPLES:
                 turned_pt = turn_features(n + 2)

@@ -16,7 +16,8 @@ ATT = 128
 TILES = TOKENS // P
 PASSES = CHANNELS // (P * PACK)
 HALVES = 2
-XT_BANKS = 2
+TURN_BANKS = 3
+AHEAD = 2
 VECTOR_ROWS = 320
 GPSIMD_STEP = 64
 RUN = 2
@@ -32,28 +33,33 @@ def tile_vc_interaction_sa_module_pa_kernel(tc, x, W_psi, b_psi, x_phi, x_theta,
         name="loads", bufs=SAMPLES
     ) as loads, tc.tile_pool(name="work", bufs=2) as work, tc.psum_pool(
         name="psum_one", bufs=1
-    ) as psum_one, tc.psum_pool(name="psum_xt", bufs=XT_BANKS) as psum_xt, tc.psum_pool(
+    ) as psum_one, tc.psum_pool(name="psum_turn", bufs=TURN_BANKS) as psum_turn, tc.psum_pool(
         name="psum_sc", bufs=TILES
     ) as psum_sc, tc.manual_schedule():
         theta_in, phi_in, x_in = [], [], []
         w_sb = const.tile([P, CHANNELS], BF16)
         bias_bc = const.tile([P, ATT], BF16)
-        for n in range(SAMPLES):
-            phi_sb = loads.tile([P, TILES, ATT], BF16)
+        def load_features(n):
+            phi_sb = loads.tile([P, TILES, ATT], BF16, name="phi_sb")
             nc.sync.dma_start(out=phi_sb[:], in_=x_phi[n].rearrange("(p t) a -> p t a", t=TILES))
-            theta_sb = loads.tile([P, TILES, ATT], BF16)
+            phi_in.append(phi_sb)
+            theta_sb = loads.tile([P, TILES, ATT], BF16, name="theta_sb")
             nc.sync.dma_start(out=theta_sb[:], in_=x_theta[n].rearrange("(p t) a -> p t a", t=TILES))
-            if n == 1:
-                nc.sync.dma_start(out=w_sb[:], in_=W_psi)
-                nc.sync.dma_start(out=bias_bc[:], in_=b_psi.partition_broadcast(P))
+            theta_in.append(theta_sb)
+
+        load_features(0)
+        for n in range(SAMPLES):
+            if n + 1 < SAMPLES:
+                load_features(n + 1)
             x_sb = loads.tile([P, TILES, CHANNELS], BF16)
             x_rows = x[n].rearrange("(p t) c -> p t c", t=TILES)
             step = TILES // 2 if n == 0 else TILES
             for first in range(0, TILES, step):
                 nc.sync.dma_start(out=x_sb[:, first : first + step, :], in_=x_rows[:, first : first + step, :])
-            theta_in.append(theta_sb)
-            phi_in.append(phi_sb)
             x_in.append(x_sb)
+            if n == 0:
+                nc.sync.dma_start(out=w_sb[:], in_=W_psi)
+                nc.sync.dma_start(out=bias_bc[:], in_=b_psi.partition_broadcast(P))
 
         ident_bf = const.tile([P, P], BF16)
         nc.vector.memset(ident_bf[:], 0.0)
@@ -72,7 +78,7 @@ def tile_vc_interaction_sa_module_pa_kernel(tc, x, W_psi, b_psi, x_phi, x_theta,
 
         def turn_channels(rows_bf16):
             words = rows_bf16.bitcast(F32)
-            turned = psum_xt.tile([P, PASSES, HALVES, P], F32, name="turned", tag="turned")
+            turned = psum_turn.tile([P, PASSES, HALVES, P], F32, name="turned", tag="turned")
             for g in range(PASSES):
                 for u in range(HALVES):
                     k = g * HALVES + u
@@ -95,14 +101,14 @@ def tile_vc_interaction_sa_module_pa_kernel(tc, x, W_psi, b_psi, x_phi, x_theta,
                 nc.tensor.transpose(out=turned[:, t, :], in_=rows[:, t, :], identity=ident_bf[:])
 
         def turn_features(n):
-            turned_pt = psum_one.tile([P, 2 * TILES, P], BF16, name="turned_pt", tag="turned_pt")
+            turned_pt = psum_turn.tile([P, 2 * TILES, P], BF16, name="turned_pt", tag="turned")
             turn_tokens(theta_in[n][:], turned_pt[:, :TILES, :])
             turn_tokens(phi_in[n][:], turned_pt[:, TILES:, :])
             return turned_pt
 
-        def copy_features(n, turned_pt):
+        def copy_features(copy, n, turned_pt):
             features[n] = work.tile([P, 2 * TILES, P], BF16, name="features")
-            nc.scalar.copy(out=features[n][:], in_=turned_pt[:])
+            copy(out=features[n][:], in_=turned_pt[:])
 
         def score_tiles(n):
             for t in range(TILES):
@@ -164,8 +170,8 @@ def tile_vc_interaction_sa_module_pa_kernel(tc, x, W_psi, b_psi, x_phi, x_theta,
         def quantise_x(n):
             x_codes[n] = work.tile([P, TILES, PASSES, P], U32, align_bytes=64, name="x_codes")
             x_scales[n] = work.tile([P, TILES, PASSES, P], U8, align_bytes=64, name="x_scales")
-            for first in range(0, TILES, XT_BANKS):
-                pair = slice(first, first + XT_BANKS)
+            for first in range(0, TILES, TILES // 2):
+                pair = slice(first, first + TILES // 2)
                 nc.vector.quantize_mx(
                     out=x_codes[n][:, pair].rearrange("q t g r -> q (t g r)").bitcast(FP8X4),
                     scales=x_scales[n][:, pair].rearrange("q t g r -> q (t g r)"),
@@ -221,9 +227,9 @@ def tile_vc_interaction_sa_module_pa_kernel(tc, x, W_psi, b_psi, x_phi, x_theta,
             nc.sync.dma_start(out=out_rows[:, tiles.start : tiles.stop, :], in_=out_sb[:])
 
         features[0] = work.tile([P, 2 * TILES, P], BF16, name="features")
-        phi_turned = psum_xt.tile([P, TILES, P], BF16, name="phi_turned", tag="turned")
-        first_turned = psum_xt.tile([P, 1, P], BF16, name="first_turned", tag="turned")
-        rest_turned = psum_one.tile([P, TILES - 1, P], BF16, name="rest_turned", tag="turned_pt")
+        phi_turned = psum_turn.tile([P, TILES, P], BF16, name="phi_turned", tag="turned")
+        first_turned = psum_turn.tile([P, 1, P], BF16, name="first_turned", tag="turned")
+        rest_turned = psum_turn.tile([P, TILES - 1, P], BF16, name="rest_turned", tag="turned")
         turn_tokens(phi_in[0][:], phi_turned[:])
         nc.vector.tensor_copy(out=features[0][:, TILES:, :], in_=phi_turned[:])
         turn_tokens(theta_in[0][:, :1, :], first_turned[:])
@@ -232,19 +238,20 @@ def tile_vc_interaction_sa_module_pa_kernel(tc, x, W_psi, b_psi, x_phi, x_theta,
         nc.scalar.copy(out=features[0][:, 1:TILES, :], in_=rest_turned[:])
         score_tiles(0)
         exponentials(0)
-        for t in range(XT_BANKS):
-            turn_x(0, t)
         turned_pt = turn_features(1)
-        copy_features(1, turned_pt)
+        copy_features(nc.vector.tensor_copy, 1, turned_pt)
+        for t in range(AHEAD):
+            turn_x(0, t)
         group_x(nc.vector.tensor_copy, 0, 0)
-        w_turned = turn_channels(w_sb[:])
+        group_x(nc.scalar.copy, 0, 1)
+        turn_x(0, 2)
         score_tiles(1)
+        w_turned = turn_channels(w_sb[:])
+        turn_x(0, 3)
+        group_x(nc.scalar.copy, 0, 2)
         w_grouped = const.tile([P, PASSES, ATT, PACK], BF16, align_bytes=64)
         group_channels(nc.scalar.copy, w_turned, w_grouped[:].bitcast(F32))
-        group_x(nc.vector.tensor_copy, 0, 1)
-        for t in range(XT_BANKS, TILES):
-            turn_x(0, t)
-            group_x(nc.scalar.copy, 0, t)
+        group_x(nc.scalar.copy, 0, 3)
         w_codes = const.tile([P, PASSES, ATT], U32, align_bytes=64)
         w_scales = const.tile([P, PASSES, ATT], U8, align_bytes=64)
 
@@ -270,7 +277,7 @@ def tile_vc_interaction_sa_module_pa_kernel(tc, x, W_psi, b_psi, x_phi, x_theta,
                 normalise(nc.gpsimd, n, inv_gpsimd, slice(first, first + GPSIMD_STEP))
             if n + 2 < SAMPLES:
                 turned_pt = turn_features(n + 2)
-            for t in range(XT_BANKS):
+            for t in range(AHEAD):
                 turn_x(n + 1, t)
             exponentials(n + 1)
             if n == 0:
@@ -279,13 +286,16 @@ def tile_vc_interaction_sa_module_pa_kernel(tc, x, W_psi, b_psi, x_phi, x_theta,
             project(n)
             quantise_cov(n, everything)
             add_bias(n)
+            group_x(nc.scalar.copy, n + 1, 0)
+            turn_x(n + 1, 2)
             if n + 2 < SAMPLES:
-                copy_features(n + 2, turned_pt)
+                copy_features(nc.scalar.copy, n + 2, turned_pt)
+            group_x(nc.scalar.copy, n + 1, 1)
+            turn_x(n + 1, 3)
+            if n + 2 < SAMPLES:
                 score_tiles(n + 2)
-            for t in range(TILES):
-                group_x(nc.scalar.copy, n + 1, t)
-                if t + XT_BANKS < TILES:
-                    turn_x(n + 1, t + XT_BANKS)
+            group_x(nc.scalar.copy, n + 1, 2)
+            group_x(nc.scalar.copy, n + 1, 3)
 
         n = SAMPLES - 1
         inv_vector = invert_sums(n, "vector")
@@ -302,5 +312,5 @@ def tile_vc_interaction_sa_module_pa_kernel(tc, x, W_psi, b_psi, x_phi, x_theta,
         quantise_cov(n, second_half)
         for half, copy in ((0, nc.scalar.copy), (1, nc.vector.tensor_copy)):
             tiles = range(half * TILES // 2, (half + 1) * TILES // 2)
-            half_acc = psum_xt.tile([P, TILES // 2, ATT], F32, name="half_acc", tag="turned")
+            half_acc = psum_turn.tile([P, TILES // 2, ATT], F32, name="half_acc", tag="turned")
             combine_and_store(n, tiles, half_acc, copy)

@@ -121,11 +121,13 @@ def tile_vc_interaction_sa_module_pa_kernel(tc, x, W_psi, b_psi, x_phi, x_theta,
                     stop=True,
                 )
 
-        def exponentials(n):
+        def exponentials(n, store_between=None):
             neg_max[n] = work.tile([P, TILES], F32, name="neg_max")
             col_sum[n] = work.tile([P, TILES], F32, name="col_sum")
             expo[n] = work.tile([P, TILES, TOKENS], F32, name="expo")
             for t in range(TILES):
+                if t == TILES // 2 and store_between is not None:
+                    store_between()
                 nc.vector.tensor_reduce(
                     out=neg_max[n][:, t : t + 1],
                     in_=scores[n, t][:],
@@ -210,7 +212,7 @@ def tile_vc_interaction_sa_module_pa_kernel(tc, x, W_psi, b_psi, x_phi, x_theta,
                 in_=x3_grouped[n][:].rearrange("p a t -> p (a t)"),
             )
 
-        def combine_and_store(n, tiles, out_acc, copy):
+        def combine(n, tiles, out_acc):
             for m in tiles:
                 nc.tensor.matmul_mx(
                     out=out_acc[:, m - tiles.start, :],
@@ -221,6 +223,8 @@ def tile_vc_interaction_sa_module_pa_kernel(tc, x, W_psi, b_psi, x_phi, x_theta,
                     start=True,
                     stop=True,
                 )
+
+        def store(n, tiles, out_acc, copy):
             out_sb = work.tile([P, len(tiles), ATT], F32, name="out_sb")
             copy(out=out_sb[:], in_=out_acc[:])
             out_rows = out[n].rearrange("(r m) a -> r m a", m=TILES)
@@ -270,7 +274,7 @@ def tile_vc_interaction_sa_module_pa_kernel(tc, x, W_psi, b_psi, x_phi, x_theta,
             if n > 0:
                 quantise_x3(n - 1)
                 out_acc = psum_one.tile([P, TILES, ATT], F32, name="out_acc", tag="acc")
-                combine_and_store(n - 1, range(TILES), out_acc, nc.scalar.copy)
+                combine(n - 1, range(TILES), out_acc)
             normalise(nc.vector, n, inv_vector, vector_share)
             inv_gpsimd = invert_sums(n, "gpsimd")
             for first in range(gpsimd_share.start, gpsimd_share.stop, GPSIMD_STEP):
@@ -279,29 +283,32 @@ def tile_vc_interaction_sa_module_pa_kernel(tc, x, W_psi, b_psi, x_phi, x_theta,
                 turned_pt = turn_features(n + 2)
             for t in range(AHEAD):
                 turn_x(n + 1, t)
-            exponentials(n + 1)
+            if n > 0:
+                exponentials(n + 1, lambda: store(n - 1, range(TILES), out_acc, nc.scalar.copy))
+            else:
+                exponentials(n + 1)
             if n == 0:
                 quantise_w()
             quantise_x(n)
             project(n)
             quantise_cov(n, everything)
             add_bias(n)
-            group_x(nc.scalar.copy, n + 1, 0)
-            turn_x(n + 1, 2)
             if n + 2 < SAMPLES:
                 copy_features(nc.scalar.copy, n + 2, turned_pt)
-            group_x(nc.scalar.copy, n + 1, 1)
+            turn_x(n + 1, 2)
+            group_x(nc.scalar.copy, n + 1, 0)
             turn_x(n + 1, 3)
             if n + 2 < SAMPLES:
                 score_tiles(n + 2)
-            group_x(nc.scalar.copy, n + 1, 2)
-            group_x(nc.scalar.copy, n + 1, 3)
+            for t in range(1, TILES):
+                group_x(nc.scalar.copy, n + 1, t)
 
         n = SAMPLES - 1
         inv_vector = invert_sums(n, "vector")
         quantise_x3(n - 1)
         out_acc = psum_one.tile([P, TILES, ATT], F32, name="out_acc", tag="acc")
-        combine_and_store(n - 1, range(TILES), out_acc, nc.scalar.copy)
+        combine(n - 1, range(TILES), out_acc)
+        store(n - 1, range(TILES), out_acc, nc.scalar.copy)
         normalise(nc.vector, n, inv_vector, first_half)
         quantise_x(n)
         project(n)
@@ -313,4 +320,5 @@ def tile_vc_interaction_sa_module_pa_kernel(tc, x, W_psi, b_psi, x_phi, x_theta,
         for half, copy in ((0, nc.scalar.copy), (1, nc.vector.tensor_copy)):
             tiles = range(half * TILES // 2, (half + 1) * TILES // 2)
             half_acc = psum_turn.tile([P, TILES // 2, ATT], F32, name="half_acc", tag="turned")
-            combine_and_store(n, tiles, half_acc, copy)
+            combine(n, tiles, half_acc)
+            store(n, tiles, half_acc, copy)

import concourse.mybir as mybir
from concourse.masks import make_identity

F32 = mybir.dt.float32
BF16 = mybir.dt.bfloat16
U32 = mybir.dt.uint32
U8 = mybir.dt.uint8
FP8X4 = mybir.dt.float8_e4m3fn_x4

P = 128
PACK = 4
SAMPLES = 4
TOKENS = 512
CHANNELS = 1024
ATT = 128
TILES = TOKENS // P
PASSES = CHANNELS // (P * PACK)
HALVES = 2
TURN_BANKS = 3
AHEAD = 2
VECTOR_ROWS = 320
GPSIMD_STEP = 64
RUN = 2

FLOPS = 2 * SAMPLES * TOKENS * ATT * (CHANNELS + 2 * TOKENS)


def tile_vc_interaction_sa_module_pa_kernel(tc, x, W_psi, b_psi, x_phi, x_theta, out):
    nc = tc.nc
    Exp = mybir.ActivationFunctionType.Exp

    with tc.tile_pool(name="const", bufs=1) as const, tc.tile_pool(
        name="loads", bufs=SAMPLES
    ) as loads, tc.tile_pool(name="work", bufs=2) as work, tc.psum_pool(
        name="psum_one", bufs=1
    ) as psum_one, tc.psum_pool(name="psum_turn", bufs=TURN_BANKS) as psum_turn, tc.psum_pool(
        name="psum_sc", bufs=TILES
    ) as psum_sc, tc.manual_schedule():
        theta_in, phi_in, x_in = [], [], []
        w_sb = const.tile([P, CHANNELS], BF16)
        bias_bc = const.tile([P, ATT], BF16)
        def load_features(n):
            phi_sb = loads.tile([P, TILES, ATT], BF16, name="phi_sb")
            nc.sync.dma_start(out=phi_sb[:], in_=x_phi[n].rearrange("(p t) a -> p t a", t=TILES))
            phi_in.append(phi_sb)
            theta_sb = loads.tile([P, TILES, ATT], BF16, name="theta_sb")
            nc.sync.dma_start(out=theta_sb[:], in_=x_theta[n].rearrange("(p t) a -> p t a", t=TILES))
            theta_in.append(theta_sb)

        load_features(0)
        for n in range(SAMPLES):
            if n + 1 < SAMPLES:
                load_features(n + 1)
            x_sb = loads.tile([P, TILES, CHANNELS], BF16)
            x_rows = x[n].rearrange("(p t) c -> p t c", t=TILES)
            step = TILES // 2 if n == 0 else TILES
            for first in range(0, TILES, step):
                nc.sync.dma_start(out=x_sb[:, first : first + step, :], in_=x_rows[:, first : first + step, :])
            x_in.append(x_sb)
            if n == 0:
                nc.sync.dma_start(out=w_sb[:], in_=W_psi)
                nc.sync.dma_start(out=bias_bc[:], in_=b_psi.partition_broadcast(P))

        ident_bf = const.tile([P, P], BF16)
        nc.vector.memset(ident_bf[:], 0.0)
        make_identity(nc, ident_bf[:], nomemset=True)
        ident_f32 = const.tile([P, P], F32)
        nc.vector.tensor_copy(out=ident_f32[:], in_=ident_bf[:])
        warm_in = const.tile([P, 1], F32)
        nc.vector.memset(warm_in[:], 0.0)
        warm_out = const.tile([P, 1], F32)
        nc.scalar.activation(out=warm_out[:], in_=warm_in[:], func=Exp)

        features, scores, neg_max, col_sum, expo = {}, {}, {}, {}, {}
        cov_grouped, cov_codes, cov_scales = {}, {}, {}
        x_turned, x_grouped, x_codes, x_scales = {}, {}, {}, {}
        x3_acc, x3_grouped, x3_codes, x3_scales = {}, {}, {}, {}

        def turn_channels(rows_bf16):
            words = rows_bf16.bitcast(F32)
            turned = psum_turn.tile([P, PASSES, HALVES, P], F32, name="turned", tag="turned")
            for g in range(PASSES):
                for u in range(HALVES):
                    k = g * HALVES + u
                    nc.tensor.transpose(out=turned[:, g, u, :], in_=words[:, k * P : (k + 1) * P], identity=ident_f32[:])
            return turned

        def group_channels(copy, turned, grouped_words):
            copy(out=grouped_words, in_=turned[:].rearrange("q g u r -> q g r u"))

        def turn_x(n, t):
            x_turned[n, t] = turn_channels(x_in[n][:, t, :])

        def group_x(copy, n, t):
            if n not in x_grouped:
                x_grouped[n] = work.tile([P, TILES, PASSES, P, PACK], BF16, align_bytes=64, name="x_grouped")
            group_channels(copy, x_turned[n, t], x_grouped[n][:].bitcast(F32)[:, t])

        def turn_tokens(rows, turned):
            for t in range(rows.shape[1]):
                nc.tensor.transpose(out=turned[:, t, :], in_=rows[:, t, :], identity=ident_bf[:])

        def turn_features(n):
            turned_pt = psum_turn.tile([P, 2 * TILES, P], BF16, name="turned_pt", tag="turned")
            turn_tokens(theta_in[n][:], turned_pt[:, :TILES, :])
            turn_tokens(phi_in[n][:], turned_pt[:, TILES:, :])
            return turned_pt

        def copy_features(copy, n, turned_pt):
            features[n] = work.tile([P, 2 * TILES, P], BF16, name="features")
            copy(out=features[n][:], in_=turned_pt[:])

        def score_tiles(n):
            for t in range(TILES):
                scores[n, t] = psum_sc.tile([P, TOKENS], F32, name="scores")
                nc.tensor.matmul(
                    out=scores[n, t][:],
                    lhsT=features[n][:, t, :],
                    rhs=features[n][:, TILES:, :].rearrange("a m r -> a (m r)"),
                    start=True,
                    stop=True,
                )

        def exponentials(n, store_between=None):
            neg_max[n] = work.tile([P, TILES], F32, name="neg_max")
            col_sum[n] = work.tile([P, TILES], F32, name="col_sum")
            expo[n] = work.tile([P, TILES, TOKENS], F32, name="expo")
            for t in range(TILES):
                if t == TILES // 2 and store_between is not None:
                    store_between()
                nc.vector.tensor_reduce(
                    out=neg_max[n][:, t : t + 1],
                    in_=scores[n, t][:],
                    axis=mybir.AxisListType.X,
                    op=mybir.AluOpType.max,
                    negate=True,
                )
                nc.scalar.activation(
                    out=expo[n][:, t, :],
                    in_=scores[n, t][:],
                    func=Exp,
                    bias=neg_max[n][:, t : t + 1],
                    scale=1.0,
                    accum_out=col_sum[n][:, t : t + 1],
                )

        def invert_sums(n, reader):
            inv_sum = work.tile([P, TILES], F32, name="inv_sum_" + reader)
            nc.vector.reciprocal(out=inv_sum[:], in_=col_sum[n][:])
            return inv_sum

        def normalise(engine, n, inv_sum, rows):
            if n not in cov_grouped:
                cov_grouped[n] = work.tile([P, TOKENS, PACK], BF16, align_bytes=64, name="cov_grouped")
            engine.tensor_tensor(
                out=cov_grouped[n][:, rows, :].rearrange("p (c i) t -> p c t i", i=RUN),
                in0=expo[n][:, :, rows].rearrange("p t (c i) -> p c t i", i=RUN),
                in1=inv_sum[:].unsqueeze(1).unsqueeze(3).to_broadcast([P, (rows.stop - rows.start) // RUN, PACK, RUN]),
                op=mybir.AluOpType.mult,
            )

        def quantise_cov(n, rows):
            if n not in cov_codes:
                cov_codes[n] = work.tile([P, TOKENS], U32, align_bytes=64, name="cov_codes")
                cov_scales[n] = work.tile([P, TOKENS], U8, align_bytes=64, name="cov_scales")
            nc.vector.quantize_mx(
                out=cov_codes[n][:, rows].bitcast(FP8X4),
                scales=cov_scales[n][:, rows],
                in_=cov_grouped[n][:, rows, :].rearrange("p i t -> p (i t)"),
            )

        def quantise_x(n):
            x_codes[n] = work.tile([P, TILES, PASSES, P], U32, align_bytes=64, name="x_codes")
            x_scales[n] = work.tile([P, TILES, PASSES, P], U8, align_bytes=64, name="x_scales")
            for first in range(0, TILES, TILES // 2):
                pair = slice(first, first + TILES // 2)
                nc.vector.quantize_mx(
                    out=x_codes[n][:, pair].rearrange("q t g r -> q (t g r)").bitcast(FP8X4),
                    scales=x_scales[n][:, pair].rearrange("q t g r -> q (t g r)"),
                    in_=x_grouped[n][:, pair].rearrange("q t g r v -> q (t g r v)"),
                )

        def project(n):
            x3_acc[n] = psum_one.tile([P, TILES, ATT], F32, name="x3_acc", tag="acc")
            for t in range(TILES):
                for g in range(PASSES):
                    nc.tensor.matmul_mx(
                        out=x3_acc[n][:, t, :],
                        lhsT=x_codes[n][:, t, g, :].bitcast(FP8X4),
                        lhsT_scale=x_scales[n][:, t, g, :],
                        rhs=w_codes[:, g, :].bitcast(FP8X4),
                        rhs_scale=w_scales[:, g, :],
                        start=(g == 0),
                        stop=(g == PASSES - 1),
                    )

        def add_bias(n):
            x3_grouped[n] = work.tile([P, ATT, PACK], BF16, align_bytes=64, name="x3_grouped")
            nc.vector.tensor_tensor(
                out=x3_grouped[n][:],
                in0=x3_acc[n][:].rearrange("p t a -> p a t"),
                in1=bias_bc[:].unsqueeze(2).to_broadcast([P, ATT, PACK]),
                op=mybir.AluOpType.add,
            )

        def quantise_x3(n):
            x3_codes[n] = work.tile([P, ATT], U32, align_bytes=64, name="x3_codes")
            x3_scales[n] = work.tile([P, ATT], U8, align_bytes=64, name="x3_scales")
            nc.vector.quantize_mx(
                out=x3_codes[n][:].bitcast(FP8X4),
                scales=x3_scales[n][:],
                in_=x3_grouped[n][:].rearrange("p a t -> p (a t)"),
            )

        def combine(n, tiles, out_acc):
            for m in tiles:
                nc.tensor.matmul_mx(
                    out=out_acc[:, m - tiles.start, :],
                    lhsT=cov_codes[n][:, m * P : (m + 1) * P].bitcast(FP8X4),
                    lhsT_scale=cov_scales[n][:, m * P : (m + 1) * P],
                    rhs=x3_codes[n][:].bitcast(FP8X4),
                    rhs_scale=x3_scales[n][:],
                    start=True,
                    stop=True,
                )

        def store(n, tiles, out_acc, copy):
            out_sb = work.tile([P, len(tiles), ATT], F32, name="out_sb")
            copy(out=out_sb[:], in_=out_acc[:])
            out_rows = out[n].rearrange("(r m) a -> r m a", m=TILES)
            nc.sync.dma_start(out=out_rows[:, tiles.start : tiles.stop, :], in_=out_sb[:])

        features[0] = work.tile([P, 2 * TILES, P], BF16, name="features")
        phi_turned = psum_turn.tile([P, TILES, P], BF16, name="phi_turned", tag="turned")
        first_turned = psum_turn.tile([P, 1, P], BF16, name="first_turned", tag="turned")
        rest_turned = psum_turn.tile([P, TILES - 1, P], BF16, name="rest_turned", tag="turned")
        turn_tokens(phi_in[0][:], phi_turned[:])
        nc.vector.tensor_copy(out=features[0][:, TILES:, :], in_=phi_turned[:])
        turn_tokens(theta_in[0][:, :1, :], first_turned[:])
        nc.scalar.copy(out=features[0][:, :1, :], in_=first_turned[:])
        turn_tokens(theta_in[0][:, 1:, :], rest_turned[:])
        nc.scalar.copy(out=features[0][:, 1:TILES, :], in_=rest_turned[:])
        score_tiles(0)
        exponentials(0)
        turned_pt = turn_features(1)
        copy_features(nc.vector.tensor_copy, 1, turned_pt)
        for t in range(AHEAD):
            turn_x(0, t)
        group_x(nc.vector.tensor_copy, 0, 0)
        group_x(nc.scalar.copy, 0, 1)
        turn_x(0, 2)
        score_tiles(1)
        w_turned = turn_channels(w_sb[:])
        turn_x(0, 3)
        group_x(nc.scalar.copy, 0, 2)
        w_grouped = const.tile([P, PASSES, ATT, PACK], BF16, align_bytes=64)
        group_channels(nc.scalar.copy, w_turned, w_grouped[:].bitcast(F32))
        group_x(nc.scalar.copy, 0, 3)
        w_codes = const.tile([P, PASSES, ATT], U32, align_bytes=64)
        w_scales = const.tile([P, PASSES, ATT], U8, align_bytes=64)

        def quantise_w():
            nc.vector.quantize_mx(
                out=w_codes[:].rearrange("q g a -> q (g a)").bitcast(FP8X4),
                scales=w_scales[:].rearrange("q g a -> q (g a)"),
                in_=w_grouped[:].rearrange("q g a v -> q (g a v)"),
            )

        everything = slice(0, TOKENS)
        first_half, second_half = slice(0, TOKENS // 2), slice(TOKENS // 2, TOKENS)
        vector_share, gpsimd_share = slice(0, VECTOR_ROWS), slice(VECTOR_ROWS, TOKENS)
        for n in range(SAMPLES - 1):
            inv_vector = invert_sums(n, "vector")
            if n > 0:
                quantise_x3(n - 1)
                out_acc = psum_one.tile([P, TILES, ATT], F32, name="out_acc", tag="acc")
                combine(n - 1, range(TILES), out_acc)
            normalise(nc.vector, n, inv_vector, vector_share)
            inv_gpsimd = invert_sums(n, "gpsimd")
            for first in range(gpsimd_share.start, gpsimd_share.stop, GPSIMD_STEP):
                normalise(nc.gpsimd, n, inv_gpsimd, slice(first, first + GPSIMD_STEP))
            if n + 2 < SAMPLES:
                turned_pt = turn_features(n + 2)
            for t in range(AHEAD):
                turn_x(n + 1, t)
            if n > 0:
                exponentials(n + 1, lambda: store(n - 1, range(TILES), out_acc, nc.scalar.copy))
            else:
                exponentials(n + 1)
            if n == 0:
                quantise_w()
            quantise_x(n)
            project(n)
            quantise_cov(n, everything)
            add_bias(n)
            if n + 2 < SAMPLES:
                copy_features(nc.scalar.copy, n + 2, turned_pt)
            turn_x(n + 1, 2)
            group_x(nc.scalar.copy, n + 1, 0)
            turn_x(n + 1, 3)
            if n + 2 < SAMPLES:
                score_tiles(n + 2)
            for t in range(1, TILES):
                group_x(nc.scalar.copy, n + 1, t)

        n = SAMPLES - 1
        inv_vector = invert_sums(n, "vector")
        quantise_x3(n - 1)
        out_acc = psum_one.tile([P, TILES, ATT], F32, name="out_acc", tag="acc")
        combine(n - 1, range(TILES), out_acc)
        store(n - 1, range(TILES), out_acc, nc.scalar.copy)
        normalise(nc.vector, n, inv_vector, first_half)
        quantise_x(n)
        project(n)
        normalise(nc.vector, n, inv_vector, second_half)
        add_bias(n)
        quantise_cov(n, first_half)
        quantise_x3(n)
        quantise_cov(n, second_half)
        for half, copy in ((0, nc.scalar.copy), (1, nc.vector.tensor_copy)):
            tiles = range(half * TILES // 2, (half + 1) * TILES // 2)
            half_acc = psum_turn.tile([P, TILES // 2, ATT], F32, name="half_acc", tag="turned")
            combine(n, tiles, half_acc)
            store(n, tiles, half_acc, copy)
